import numpy as np
import ml_dtypes


def mxq(x, axis, fmt="e4m3"):
    dtype, down = {"e4m3": (ml_dtypes.float8_e4m3fn, 7), "e5m2": (ml_dtypes.float8_e5m2, 14)}[fmt]
    v = np.moveaxis(np.asarray(x, np.float32).astype(ml_dtypes.bfloat16).astype(np.float64), axis, -1)
    blocks = v.reshape(v.shape[:-1] + (-1, 32))
    amax = np.abs(blocks).max(-1, keepdims=True)
    byte = np.maximum(np.where(amax > 0, np.frexp(amax)[1] - 1 + 127, 0) - down, 1)
    scale = np.exp2(byte - 127.0)
    codes = (blocks / scale).astype(np.float32).astype(dtype).astype(np.float64)
    return np.moveaxis((codes * scale).reshape(v.shape), -1, axis)


WIDE = False


def mx_kscale(k):
    if not WIDE:
        return np.ones(k)
    levels = np.array([10, -10, 5, -5, 0])
    if k % 512:
        return np.exp2(np.random.permutation(np.resize(levels, k // 32))).repeat(32)
    a = np.empty((k // 512, 16))
    for p in range(k // 512):
        a[p, :8] = np.random.permutation(np.resize(levels, 8))
        for g in range(8):
            far = levels[np.abs(levels - a[p, g]) >= 10]
            a[p, g + 8] = far[np.random.randint(len(far))]
    return np.exp2(a.ravel()).repeat(32)


BF16 = ml_dtypes.bfloat16


def bf(x):
    return np.asarray(x, np.float32).astype(BF16)


def f64(x):
    return np.asarray(x).astype(np.float64)


BATCH, SEQ, IN_DIM, MID_DIM, OUT_DIM = 2, 64, 1024, 1024, 512
CB = 2.0 ** -np.round(np.log2(IN_DIM) / 2)
CA = 2.0 ** -np.round(np.log2(MID_DIM) / 2)


def signs(shape):
    return np.where(np.random.standard_normal(shape) >= 0, 1.0, -1.0)


def setup_inputs():
    s, t = mx_kscale(IN_DIM), mx_kscale(MID_DIM)
    return {"x": bf(np.random.standard_normal((BATCH, SEQ, IN_DIM)) * s),
            "scaling0": bf(0.5 + np.random.uniform(size=IN_DIM)),
            "B": bf(signs((MID_DIM, IN_DIM)) * CB / s[None, :]),
            "scaling2": bf((0.5 + np.random.uniform(size=MID_DIM)) * t),
            "A": bf(signs((OUT_DIM, MID_DIM)) * CA / t[None, :]),
            "scaling4": bf(0.5 + np.random.uniform(size=OUT_DIM)),
            "bias": bf(np.random.standard_normal(OUT_DIM))}


def reference(x, scaling0, B, scaling2, A, scaling4, bias):
    h = f64(x) * f64(scaling0)
    h = mxq(h, 2, "e4m3") @ mxq(f64(B), 1, "e4m3").T
    h = h * f64(scaling2)
    h = mxq(h, 2, "e4m3") @ mxq(f64(A), 1, "e4m3").T
    return h * f64(scaling4) + f64(bias)

@@ -1,0 +1,226 @@
+from contextlib import ExitStack
+
+import concourse.mybir as mybir
+from concourse.masks import make_identity
+
+BF16 = mybir.dt.bfloat16
+F32 = mybir.dt.float32
+U32 = mybir.dt.uint32
+U8 = mybir.dt.uint8
+FP8X4 = mybir.dt.float8_e4m3fn_x4
+MULT = mybir.AluOpType.mult
+ADD = mybir.AluOpType.add
+
+P = 128
+PACK = 4
+PASSES = 2
+K_DIM = 1024
+OUT_DIM = 512
+WORD_BLOCKS = 4
+CHUNK_ROWS = 2 * P
+B_CHUNKS = 4
+A_CHUNKS = 2
+TILE_WORDS = PASSES * P
+CHUNK_PASSES = 2 * PASSES
+LOOKAHEAD = 2
+WARM_PASSES = 12
+
+FLOPS = 2 * P * K_DIM * K_DIM + 2 * P * K_DIM * OUT_DIM
+
+
+def pass_cols(g):
+    return slice(g * P, (g + 1) * P)
+
+
+def transpose_row_tile(nc, banks, rows, identity):
+    words = rows.bitcast(F32)
+    bank = banks.tile([P, WORD_BLOCKS, P], F32, name="bank")
+    for g in range(PASSES):
+        for u in range(2):
+            pass_words = slice(2 * P * g + u, 2 * P * (g + 1), 2)
+            nc.tensor.transpose(bank[:, 2 * g + u, :], words[:, pass_words], identity[:])
+    return bank
+
+
+def tile_doublebinarylinear_s_kernel(tc, x, scaling0, B, scaling2, A, scaling4, bias, out):
+    nc = tc.nc
+    x_rows = x.rearrange("b s k -> (b s) k")
+    out_rows = out.rearrange("b s o -> (b s) o")
+    B_rows = B.rearrange("(g p u e) k -> g u p e k", g=PASSES, u=2, e=2)
+    A_rows = A.rearrange("(c p e) k -> c p e k", c=A_CHUNKS, e=2)
+    chunk_rows = [B_rows[c // 2, c % 2] for c in range(B_CHUNKS)] + [A_rows[c] for c in range(A_CHUNKS)]
+    chunks = len(chunk_rows)
+
+    with ExitStack() as ctx:
+        keep = ctx.enter_context(tc.tile_pool(name="keep", bufs=1))
+        stage = ctx.enter_context(tc.tile_pool(name="stage", bufs=4))
+        banks = ctx.enter_context(tc.psum_pool(name="banks", bufs=4))
+        sums = ctx.enter_context(tc.psum_pool(name="sums", bufs=1))
+        ctx.enter_context(tc.manual_schedule())
+
+        zeros = keep.tile([P, PACK * P], BF16, align_bytes=64)
+        nc.vector.memset(zeros[:].bitcast(F32), 0.0)
+        zero_codes = keep.tile([P, P], U32, align_bytes=64)
+        zero_scales = keep.tile([P, P], U8, align_bytes=64)
+        nc.vector.quantize_mx(out=zero_codes[:].bitcast(FP8X4), scales=zero_scales[:], in_=zeros[:])
+        idle_sums = sums.tile([P, P], F32)
+
+        def idle_passes(count):
+            for w in range(count):
+                nc.tensor.matmul_mx(
+                    out=idle_sums[:],
+                    lhsT=zero_codes[:].bitcast(FP8X4),
+                    lhsT_scale=zero_scales[:],
+                    rhs=zero_codes[:].bitcast(FP8X4),
+                    rhs_scale=zero_scales[:],
+                    start=(w == 0),
+                    stop=(w == count - 1),
+                )
+
+        idle_passes(WARM_PASSES)
+
+        identity = keep.tile([P, P], F32)
+        make_identity(nc, identity[:])
+        row_zero = keep.tile([P, 2 * OUT_DIM], BF16)
+        nc.vector.memset(row_zero[:].bitcast(F32), 0.0)
+        ones = keep.tile([P, P], BF16)
+        nc.vector.memset(ones[:], 1.0)
+
+        s0_cols = keep.tile([P, 2 * WORD_BLOCKS], BF16)
+        s2_cols = keep.tile([P, 2 * WORD_BLOCKS], BF16)
+        for s_cols, scaling in ((s0_cols, scaling0), (s2_cols, scaling2)):
+            nc.scalar.dma_start(
+                out=s_cols[:].rearrange("p (g t) -> p g t", t=PACK),
+                in_=scaling.rearrange("(g p t) -> p g t", p=P, t=PACK),
+            )
+        nc.scalar.dma_start(out=row_zero[0:1, 0:OUT_DIM], in_=scaling4.unsqueeze(0))
+        nc.scalar.dma_start(out=row_zero[0:1, OUT_DIM : 2 * OUT_DIM], in_=bias.unsqueeze(0))
+        x_sb = keep.tile([P, K_DIM], BF16)
+        nc.sync.dma_start(out=x_sb[:], in_=x_rows)
+        w_sb = []
+        for i in range(chunks):
+            chunk = keep.tile([P, 2, K_DIM], BF16, name="w_sb%d" % i)
+            rows = chunk_rows[i]
+            if i < chunks - 1:
+                nc.sync.dma_start(out=chunk[:], in_=rows)
+            else:
+                for e in range(2):
+                    nc.sync.dma_start(out=chunk[:, e, :], in_=rows[:, e, :])
+            w_sb.append(chunk)
+
+        x_bank = transpose_row_tile(nc, banks, x_sb[:], identity)
+        x_halves = x_bank[:].bitcast(BF16)
+        h0_grouped = keep.tile([P, PASSES, P, PACK], BF16, align_bytes=64)
+        for g in range(PASSES):
+            nc.vector.tensor_tensor(
+                out=h0_grouped[:, g].rearrange("p r (u e) -> p r u e", e=2),
+                in0=x_halves[:, 2 * g : 2 * g + 2, :].rearrange("p u (r e) -> p r u e", e=2),
+                in1=s0_cols[:, PACK * g : PACK * (g + 1)]
+                .rearrange("p (u e) -> p u e", e=2)
+                .unsqueeze(1)
+                .to_broadcast([P, P, 2, 2]),
+                op=MULT,
+            )
+        h0_codes = keep.tile([P, TILE_WORDS], U32, align_bytes=64)
+        h0_scales = keep.tile([P, TILE_WORDS], U8, align_bytes=64)
+        nc.vector.quantize_mx(
+            out=h0_codes[:].bitcast(FP8X4),
+            scales=h0_scales[:],
+            in_=h0_grouped[:].rearrange("p g r t -> p (g r t)"),
+        )
+
+        w_codes = [keep.tile([P, 2, TILE_WORDS], U32, name="w_codes%d" % i, align_bytes=64) for i in range(chunks)]
+        w_scales = [keep.tile([P, 2, TILE_WORDS], U8, name="w_scales%d" % i, align_bytes=64) for i in range(chunks)]
+        h1 = [sums.tile([P, PACK, P], F32, name="h1_%d" % g, tag="sum%d" % g) for g in range(PASSES)]
+        h2_codes = keep.tile([P, TILE_WORDS], U32, align_bytes=64)
+        h2_scales = keep.tile([P, TILE_WORDS], U8, align_bytes=64)
+
+        def transpose_chunk(i):
+            return [transpose_row_tile(nc, banks, w_sb[i][:, e, :], identity) for e in range(2)]
+
+        def quantise_chunk(i, chunk_banks):
+            for e in range(2):
+                grouped = stage.tile([P, PASSES, P, PACK], BF16, align_bytes=64)
+                nc.scalar.copy(
+                    out=grouped[:].bitcast(F32),
+                    in_=chunk_banks[e][:].rearrange("p (g u) r -> p g r u", u=2),
+                )
+                nc.vector.quantize_mx(
+                    out=w_codes[i][:, e, :].bitcast(FP8X4),
+                    scales=w_scales[i][:, e, :],
+                    in_=grouped[:].rearrange("p g r t -> p (g r t)"),
+                )
+
+        def first_matmul(c):
+            g2, u2 = divmod(c, 2)
+            for e in range(2):
+                for g in range(PASSES):
+                    nc.tensor.matmul_mx(
+                        out=h1[g2][:, 2 * u2 + e, :],
+                        lhsT=w_codes[c][:, e, pass_cols(g)].bitcast(FP8X4),
+                        lhsT_scale=w_scales[c][:, e, pass_cols(g)],
+                        rhs=h0_codes[:, pass_cols(g)].bitcast(FP8X4),
+                        rhs_scale=h0_scales[:, pass_cols(g)],
+                        start=(g == 0),
+                        stop=(g == PASSES - 1),
+                    )
+            if u2 == 1:
+                h2_grouped = stage.tile([P, P, PACK], BF16, align_bytes=64)
+                nc.vector.tensor_tensor(
+                    out=h2_grouped[:],
+                    in0=h1[g2][:].rearrange("p t r -> p r t"),
+                    in1=s2_cols[:, PACK * g2 : PACK * (g2 + 1)].unsqueeze(1).to_broadcast([P, P, PACK]),
+                    op=MULT,
+                )
+                nc.vector.quantize_mx(
+                    out=h2_codes[:, pass_cols(g2)].bitcast(FP8X4),
+                    scales=h2_scales[:, pass_cols(g2)],
+                    in_=h2_grouped[:].rearrange("p r t -> p (r t)"),
+                )
+
+        def second_matmul(c):
+            i = B_CHUNKS + c
+            h3 = sums.tile([P, 2, P], F32, tag="sum%d" % c)
+            for e in range(2):
+                for g in range(PASSES):
+                    nc.tensor.matmul_mx(
+                        out=h3[:, e, :],
+                        lhsT=h2_codes[:, pass_cols(g)].bitcast(FP8X4),
+                        lhsT_scale=h2_scales[:, pass_cols(g)],
+                        rhs=w_codes[i][:, e, pass_cols(g)].bitcast(FP8X4),
+                        rhs_scale=w_scales[i][:, e, pass_cols(g)],
+                        start=(g == 0),
+                        stop=(g == PASSES - 1),
+                    )
+            cols = slice(c * CHUNK_ROWS, (c + 1) * CHUNK_ROWS)
+            result = stage.tile([P, CHUNK_ROWS], F32)
+            nc.vector.tensor_tensor(
+                out=result[:].rearrange("r (p e) -> r p e", e=2),
+                in0=h3[:].rearrange("r e p -> r p e"),
+                in1=s4_all[:, cols].rearrange("r (p e) -> r p e", e=2),
+                op=MULT,
+            )
+            nc.vector.tensor_tensor(out=result[:], in0=result[:], in1=bias_all[:, cols], op=ADD)
+            nc.sync.dma_start(out=out_rows[:, cols], in_=result[:])
+
+        assert chunks - LOOKAHEAD == B_CHUNKS
+        for step in range(chunks):
+            chunk_banks = transpose_chunk(step)
+            if step < LOOKAHEAD:
+                idle_passes(CHUNK_PASSES)
+            else:
+                first_matmul(step - LOOKAHEAD)
+            quantise_chunk(step, chunk_banks)
+
+        s4_bank = banks.tile([P, WORD_BLOCKS, P], F32, name="bank")
+        s4_spread = s4_bank[:].rearrange("p a b -> p (a b)")
+        nc.tensor.matmul(out=s4_spread, lhsT=ones[:], rhs=row_zero[:, 0:OUT_DIM], start=True, stop=True)
+        s4_all = keep.tile([P, OUT_DIM], F32)
+        nc.scalar.copy(out=s4_all[:], in_=s4_spread)
+        bias_all = sums.tile([P, OUT_DIM], F32)
+        nc.tensor.matmul(
+            out=bias_all[:], lhsT=ones[:], rhs=row_zero[:, OUT_DIM : 2 * OUT_DIM], start=True, stop=True
+        )
+
+        for c in range(A_CHUNKS):
+            second_matmul(c)

@@ -16,14 +16,16 @@ PACK = 4
 PASSES = 2
 K_DIM = 1024
 OUT_DIM = 512
-WORD_BLOCKS = 4
-CHUNK_ROWS = 2 * P
-B_CHUNKS = 4
-A_CHUNKS = 2
+B_TILES = 8
+A_TILES = 4
+TILES = B_TILES + A_TILES
 TILE_WORDS = PASSES * P
-CHUNK_PASSES = 2 * PASSES
-LOOKAHEAD = 2
-WARM_PASSES = 12
+STORE_TILES = 2
+
+X_BEFORE = 3
+SCALINGS_BEFORE = 5
+ROWS_BEFORE = 9
+MULTIPLY_AFTER = (6, 9)
 
 FLOPS = 2 * P * K_DIM * K_DIM + 2 * P * K_DIM * OUT_DIM
 
@@ -32,195 +34,177 @@ def pass_cols(g):
     return slice(g * P, (g + 1) * P)
 
 
-def transpose_row_tile(nc, banks, rows, identity):
-    words = rows.bitcast(F32)
-    bank = banks.tile([P, WORD_BLOCKS, P], F32, name="bank")
-    for g in range(PASSES):
-        for u in range(2):
-            pass_words = slice(2 * P * g + u, 2 * P * (g + 1), 2)
-            nc.tensor.transpose(bank[:, 2 * g + u, :], words[:, pass_words], identity[:])
-    return bank
-
-
 def tile_doublebinarylinear_s_kernel(tc, x, scaling0, B, scaling2, A, scaling4, bias, out):
     nc = tc.nc
     x_rows = x.rearrange("b s k -> (b s) k")
     out_rows = out.rearrange("b s o -> (b s) o")
-    B_rows = B.rearrange("(g p u e) k -> g u p e k", g=PASSES, u=2, e=2)
-    A_rows = A.rearrange("(c p e) k -> c p e k", c=A_CHUNKS, e=2)
-    chunk_rows = [B_rows[c // 2, c % 2] for c in range(B_CHUNKS)] + [A_rows[c] for c in range(A_CHUNKS)]
-    chunks = len(chunk_rows)
+    B_rows = B.rearrange("(g p t) k -> g t p k", g=PASSES, t=PACK)
+    w_rows = [B_rows[w // PACK, w % PACK] for w in range(B_TILES)]
+    w_rows += [A[a * P : (a + 1) * P, :] for a in range(A_TILES)]
 
     with ExitStack() as ctx:
         keep = ctx.enter_context(tc.tile_pool(name="keep", bufs=1))
         stage = ctx.enter_context(tc.tile_pool(name="stage", bufs=4))
-        banks = ctx.enter_context(tc.psum_pool(name="banks", bufs=4))
+        banks = ctx.enter_context(tc.psum_pool(name="banks", bufs=5))
         sums = ctx.enter_context(tc.psum_pool(name="sums", bufs=1))
         ctx.enter_context(tc.manual_schedule())
 
-        zeros = keep.tile([P, PACK * P], BF16, align_bytes=64)
-        nc.vector.memset(zeros[:].bitcast(F32), 0.0)
-        zero_codes = keep.tile([P, P], U32, align_bytes=64)
-        zero_scales = keep.tile([P, P], U8, align_bytes=64)
-        nc.vector.quantize_mx(out=zero_codes[:].bitcast(FP8X4), scales=zero_scales[:], in_=zeros[:])
-        idle_sums = sums.tile([P, P], F32)
-
-        def idle_passes(count):
-            for w in range(count):
-                nc.tensor.matmul_mx(
-                    out=idle_sums[:],
-                    lhsT=zero_codes[:].bitcast(FP8X4),
-                    lhsT_scale=zero_scales[:],
-                    rhs=zero_codes[:].bitcast(FP8X4),
-                    rhs_scale=zero_scales[:],
-                    start=(w == 0),
-                    stop=(w == count - 1),
-                )
-
-        idle_passes(WARM_PASSES)
-
-        identity = keep.tile([P, P], F32)
-        make_identity(nc, identity[:])
-        row_zero = keep.tile([P, 2 * OUT_DIM], BF16)
-        nc.vector.memset(row_zero[:].bitcast(F32), 0.0)
+        s4_row = keep.tile([P, OUT_DIM], BF16)
+        bias_row = keep.tile([P, OUT_DIM], BF16)
+        nc.vector.memset(s4_row[:].bitcast(F32), 0.0)
+        nc.vector.memset(bias_row[:].bitcast(F32), 0.0)
         ones = keep.tile([P, P], BF16)
         nc.vector.memset(ones[:], 1.0)
+        identity = keep.tile([P, P], F32)
+        make_identity(nc, identity[:])
 
-        s0_cols = keep.tile([P, 2 * WORD_BLOCKS], BF16)
-        s2_cols = keep.tile([P, 2 * WORD_BLOCKS], BF16)
-        for s_cols, scaling in ((s0_cols, scaling0), (s2_cols, scaling2)):
-            nc.scalar.dma_start(
-                out=s_cols[:].rearrange("p (g t) -> p g t", t=PACK),
-                in_=scaling.rearrange("(g p t) -> p g t", p=P, t=PACK),
-            )
-        nc.scalar.dma_start(out=row_zero[0:1, 0:OUT_DIM], in_=scaling4.unsqueeze(0))
-        nc.scalar.dma_start(out=row_zero[0:1, OUT_DIM : 2 * OUT_DIM], in_=bias.unsqueeze(0))
+        s0_cols = keep.tile([P, PASSES * PACK], BF16)
+        s2_cols = keep.tile([P, PASSES * PACK], BF16)
         x_sb = keep.tile([P, K_DIM], BF16)
-        nc.sync.dma_start(out=x_sb[:], in_=x_rows)
-        w_sb = []
-        for i in range(chunks):
-            chunk = keep.tile([P, 2, K_DIM], BF16, name="w_sb%d" % i)
-            rows = chunk_rows[i]
-            if i < chunks - 1:
-                nc.sync.dma_start(out=chunk[:], in_=rows)
-            else:
-                for e in range(2):
-                    nc.sync.dma_start(out=chunk[:, e, :], in_=rows[:, e, :])
-            w_sb.append(chunk)
+        w_sb = [keep.tile([P, K_DIM], BF16, name="w_sb%d" % w) for w in range(TILES)]
+        for w in range(TILES):
+            if w == X_BEFORE:
+                nc.sync.dma_start(out=x_sb[:], in_=x_rows)
+            if w == SCALINGS_BEFORE:
+                for s_cols, scaling in ((s0_cols, scaling0), (s2_cols, scaling2)):
+                    nc.scalar.dma_start(
+                        out=s_cols[:].rearrange("p (g t) -> p g t", t=PACK),
+                        in_=scaling.rearrange("(g p t) -> p g t", p=P, t=PACK),
+                    )
+            if w == ROWS_BEFORE:
+                nc.sync.dma_start(out=s4_row[0:1, :], in_=scaling4.unsqueeze(0))
+                nc.sync.dma_start(out=bias_row[0:1, :], in_=bias.unsqueeze(0))
+            nc.sync.dma_start(out=w_sb[w][:], in_=w_rows[w])
 
-        x_bank = transpose_row_tile(nc, banks, x_sb[:], identity)
-        x_halves = x_bank[:].bitcast(BF16)
-        h0_grouped = keep.tile([P, PASSES, P, PACK], BF16, align_bytes=64)
-        for g in range(PASSES):
-            nc.vector.tensor_tensor(
-                out=h0_grouped[:, g].rearrange("p r (u e) -> p r u e", e=2),
-                in0=x_halves[:, 2 * g : 2 * g + 2, :].rearrange("p u (r e) -> p r u e", e=2),
-                in1=s0_cols[:, PACK * g : PACK * (g + 1)]
-                .rearrange("p (u e) -> p u e", e=2)
-                .unsqueeze(1)
-                .to_broadcast([P, P, 2, 2]),
-                op=MULT,
-            )
+        def transpose_rows(rows):
+            words = rows.bitcast(F32)
+            bank = banks.tile([P, PASSES, 2, P], F32, name="bank")
+            for g in range(PASSES):
+                for u in range(2):
+                    pass_words = slice(2 * P * g + u, 2 * P * (g + 1), 2)
+                    nc.tensor.transpose(bank[:, g, u, :], words[:, pass_words], identity[:])
+            return bank
+
         h0_codes = keep.tile([P, TILE_WORDS], U32, align_bytes=64)
         h0_scales = keep.tile([P, TILE_WORDS], U8, align_bytes=64)
-        nc.vector.quantize_mx(
-            out=h0_codes[:].bitcast(FP8X4),
-            scales=h0_scales[:],
-            in_=h0_grouped[:].rearrange("p g r t -> p (g r t)"),
-        )
 
-        w_codes = [keep.tile([P, 2, TILE_WORDS], U32, name="w_codes%d" % i, align_bytes=64) for i in range(chunks)]
-        w_scales = [keep.tile([P, 2, TILE_WORDS], U8, name="w_scales%d" % i, align_bytes=64) for i in range(chunks)]
-        h1 = [sums.tile([P, PACK, P], F32, name="h1_%d" % g, tag="sum%d" % g) for g in range(PASSES)]
+        def make_h0():
+            x_bank = transpose_rows(x_sb[:])
+            x_pairs = x_bank[:].rearrange("p g u r -> p (g u r)").bitcast(BF16)
+            x_pairs = x_pairs.rearrange("p (g u r e) -> p g r u e", g=PASSES, u=2, e=2)
+            h0_grouped = keep.tile([P, PASSES, P, PACK], BF16, align_bytes=64)
+            for g in range(PASSES):
+                nc.vector.tensor_tensor(
+                    out=h0_grouped[:, g].rearrange("p r (u e) -> p r u e", e=2),
+                    in0=x_pairs[:, g],
+                    in1=s0_cols[:, PACK * g : PACK * (g + 1)]
+                    .rearrange("p (u e) -> p u e", e=2)
+                    .unsqueeze(1)
+                    .to_broadcast([P, P, 2, 2]),
+                    op=MULT,
+                )
+            nc.vector.quantize_mx(
+                out=h0_codes[:].bitcast(FP8X4),
+                scales=h0_scales[:],
+                in_=h0_grouped[:].rearrange("p g r t -> p (g r t)"),
+            )
+
+        w_codes = [keep.tile([P, TILE_WORDS], U32, name="w_codes%d" % w, align_bytes=64) for w in range(TILES)]
+        w_scales = [keep.tile([P, TILE_WORDS], U8, name="w_scales%d" % w, align_bytes=64) for w in range(TILES)]
+
+        def regroup(bank):
+            grouped = stage.tile([P, PASSES, P, PACK], BF16, align_bytes=64)
+            nc.scalar.copy(out=grouped[:].bitcast(F32), in_=bank[:].rearrange("p g u r -> p g r u"))
+            return grouped
+
+        def quantise(w, grouped):
+            nc.vector.quantize_mx(
+                out=w_codes[w][:].bitcast(FP8X4),
+                scales=w_scales[w][:],
+                in_=grouped[:].rearrange("p g r t -> p (g r t)"),
+            )
+
+        h1 = [sums.tile([P, PACK, P], F32, name="h1_%d" % g) for g in range(PASSES)]
         h2_codes = keep.tile([P, TILE_WORDS], U32, align_bytes=64)
         h2_scales = keep.tile([P, TILE_WORDS], U8, align_bytes=64)
 
-        def transpose_chunk(i):
-            return [transpose_row_tile(nc, banks, w_sb[i][:, e, :], identity) for e in range(2)]
-
-        def quantise_chunk(i, chunk_banks):
-            for e in range(2):
-                grouped = stage.tile([P, PASSES, P, PACK], BF16, align_bytes=64)
-                nc.scalar.copy(
-                    out=grouped[:].bitcast(F32),
-                    in_=chunk_banks[e][:].rearrange("p (g u) r -> p g r u", u=2),
-                )
-                nc.vector.quantize_mx(
-                    out=w_codes[i][:, e, :].bitcast(FP8X4),
-                    scales=w_scales[i][:, e, :],
-                    in_=grouped[:].rearrange("p g r t -> p (g r t)"),
+        def first_matmul(w):
+            for g in range(PASSES):
+                nc.tensor.matmul_mx(
+                    out=h1[w // PACK][:, w % PACK, :],
+                    lhsT=w_codes[w][:, pass_cols(g)].bitcast(FP8X4),
+                    lhsT_scale=w_scales[w][:, pass_cols(g)],
+                    rhs=h0_codes[:, pass_cols(g)].bitcast(FP8X4),
+                    rhs_scale=h0_scales[:, pass_cols(g)],
+                    start=(g == 0),
+                    stop=(g == PASSES - 1),
                 )
 
-        def first_matmul(c):
-            g2, u2 = divmod(c, 2)
-            for e in range(2):
-                for g in range(PASSES):
-                    nc.tensor.matmul_mx(
-                        out=h1[g2][:, 2 * u2 + e, :],
-                        lhsT=w_codes[c][:, e, pass_cols(g)].bitcast(FP8X4),
-                        lhsT_scale=w_scales[c][:, e, pass_cols(g)],
-                        rhs=h0_codes[:, pass_cols(g)].bitcast(FP8X4),
-                        rhs_scale=h0_scales[:, pass_cols(g)],
-                        start=(g == 0),
-                        stop=(g == PASSES - 1),
-                    )
-            if u2 == 1:
-                h2_grouped = stage.tile([P, P, PACK], BF16, align_bytes=64)
-                nc.vector.tensor_tensor(
-                    out=h2_grouped[:],
-                    in0=h1[g2][:].rearrange("p t r -> p r t"),
-                    in1=s2_cols[:, PACK * g2 : PACK * (g2 + 1)].unsqueeze(1).to_broadcast([P, P, PACK]),
-                    op=MULT,
-                )
-                nc.vector.quantize_mx(
-                    out=h2_codes[:, pass_cols(g2)].bitcast(FP8X4),
-                    scales=h2_scales[:, pass_cols(g2)],
-                    in_=h2_grouped[:].rearrange("p r t -> p (r t)"),
-                )
-
-        def second_matmul(c):
-            i = B_CHUNKS + c
-            h3 = sums.tile([P, 2, P], F32, tag="sum%d" % c)
-            for e in range(2):
-                for g in range(PASSES):
-                    nc.tensor.matmul_mx(
-                        out=h3[:, e, :],
-                        lhsT=h2_codes[:, pass_cols(g)].bitcast(FP8X4),
-                        lhsT_scale=h2_scales[:, pass_cols(g)],
-                        rhs=w_codes[i][:, e, pass_cols(g)].bitcast(FP8X4),
-                        rhs_scale=w_scales[i][:, e, pass_cols(g)],
-                        start=(g == 0),
-                        stop=(g == PASSES - 1),
-                    )
-            cols = slice(c * CHUNK_ROWS, (c + 1) * CHUNK_ROWS)
-            result = stage.tile([P, CHUNK_ROWS], F32)
+        def make_h2(g):
+            h2_grouped = stage.tile([P, P, PACK], BF16, align_bytes=64)
             nc.vector.tensor_tensor(
-                out=result[:].rearrange("r (p e) -> r p e", e=2),
-                in0=h3[:].rearrange("r e p -> r p e"),
-                in1=s4_all[:, cols].rearrange("r (p e) -> r p e", e=2),
+                out=h2_grouped[:],
+                in0=h1[g][:].rearrange("p t r -> p r t"),
+                in1=s2_cols[:, PACK * g : PACK * (g + 1)].unsqueeze(1).to_broadcast([P, P, PACK]),
                 op=MULT,
             )
-            nc.vector.tensor_tensor(out=result[:], in0=result[:], in1=bias_all[:, cols], op=ADD)
-            nc.sync.dma_start(out=out_rows[:, cols], in_=result[:])
+            nc.vector.quantize_mx(
+                out=h2_codes[:, pass_cols(g)].bitcast(FP8X4),
+                scales=h2_scales[:, pass_cols(g)],
+                in_=h2_grouped[:].rearrange("p r t -> p (r t)"),
+            )
 
-        assert chunks - LOOKAHEAD == B_CHUNKS
-        for step in range(chunks):
-            chunk_banks = transpose_chunk(step)
-            if step < LOOKAHEAD:
-                idle_passes(CHUNK_PASSES)
-            else:
-                first_matmul(step - LOOKAHEAD)
-            quantise_chunk(step, chunk_banks)
+        def second_matmul(c):
+            h3 = banks.tile([P, STORE_TILES * P], F32, name="bank")
+            for n in range(STORE_TILES):
+                w = B_TILES + STORE_TILES * c + n
+                for g in range(PASSES):
+                    nc.tensor.matmul_mx(
+                        out=h3[:, n * P : (n + 1) * P],
+                        lhsT=h2_codes[:, pass_cols(g)].bitcast(FP8X4),
+                        lhsT_scale=h2_scales[:, pass_cols(g)],
+                        rhs=w_codes[w][:, pass_cols(g)].bitcast(FP8X4),
+                        rhs_scale=w_scales[w][:, pass_cols(g)],
+                        start=(g == 0),
+                        stop=(g == PASSES - 1),
+                    )
+            return h3
 
-        s4_bank = banks.tile([P, WORD_BLOCKS, P], F32, name="bank")
-        s4_spread = s4_bank[:].rearrange("p a b -> p (a b)")
-        nc.tensor.matmul(out=s4_spread, lhsT=ones[:], rhs=row_zero[:, 0:OUT_DIM], start=True, stop=True)
+        results = [keep.tile([P, STORE_TILES * P], F32, name="result%d" % c) for c in range(A_TILES // STORE_TILES)]
+
+        def out_cols(c):
+            return slice(c * STORE_TILES * P, (c + 1) * STORE_TILES * P)
+
+        def scale_out(c, h3):
+            nc.vector.tensor_tensor(out=results[c][:], in0=h3[:], in1=s4_all[:, out_cols(c)], op=MULT)
+
+        def add_bias_and_store(c):
+            nc.vector.tensor_tensor(out=results[c][:], in0=results[c][:], in1=bias_all[:, out_cols(c)], op=ADD)
+            nc.sync.dma_start(out=out_rows[:, out_cols(c)], in_=results[c][:])
+
+        for w in range(TILES - 1):
+            if w == X_BEFORE:
+                make_h0()
+            grouped = regroup(transpose_rows(w_sb[w][:]))
+            if w == MULTIPLY_AFTER[1]:
+                for n in range(PACK):
+                    first_matmul(PACK + n)
+                make_h2(1)
+            quantise(w, grouped)
+            if w == MULTIPLY_AFTER[0]:
+                for n in range(PACK):
+                    first_matmul(n)
+                make_h2(0)
+        last_grouped = regroup(transpose_rows(w_sb[TILES - 1][:]))
+        s4_bank = banks.tile([P, OUT_DIM], F32, name="bank")
+        nc.tensor.matmul(out=s4_bank[:], lhsT=ones[:], rhs=s4_row[:], start=True, stop=True)
         s4_all = keep.tile([P, OUT_DIM], F32)
-        nc.scalar.copy(out=s4_all[:], in_=s4_spread)
+        nc.scalar.copy(out=s4_all[:], in_=s4_bank[:])
+        first_half = second_matmul(0)
         bias_all = sums.tile([P, OUT_DIM], F32)
-        nc.tensor.matmul(
-            out=bias_all[:], lhsT=ones[:], rhs=row_zero[:, OUT_DIM : 2 * OUT_DIM], start=True, stop=True
-        )
-
-        for c in range(A_CHUNKS):
-            second_matmul(c)
+        nc.tensor.matmul(out=bias_all[:], lhsT=ones[:], rhs=bias_row[:], start=True, stop=True)
+        quantise(TILES - 1, last_grouped)
+        scale_out(0, first_half)
+        add_bias_and_store(0)
+        scale_out(1, second_matmul(1))
+        add_bias_and_store(1)

@@ -26,6 +26,9 @@ X_BEFORE = 3
 SCALINGS_BEFORE = 5
 ROWS_BEFORE = 9
 MULTIPLY_AFTER = (6, 9)
+WARM_PASSES = 12
+IDLE_AFTER = (1, 2, 4, 8)
+IDLE_PASSES = 4
 
 FLOPS = 2 * P * K_DIM * K_DIM + 2 * P * K_DIM * OUT_DIM
 
@@ -51,12 +54,34 @@ def tile_doublebinarylinear_s_kernel(tc, x, scaling0, B, scaling2, A, scaling4, 
 
         s4_row = keep.tile([P, OUT_DIM], BF16)
         bias_row = keep.tile([P, OUT_DIM], BF16)
-        nc.vector.memset(s4_row[:].bitcast(F32), 0.0)
-        nc.vector.memset(bias_row[:].bitcast(F32), 0.0)
         ones = keep.tile([P, P], BF16)
-        nc.vector.memset(ones[:], 1.0)
         identity = keep.tile([P, P], F32)
         make_identity(nc, identity[:])
+
+        zeros = keep.tile([P, PACK * P], BF16, align_bytes=64)
+        nc.vector.memset(zeros[:].bitcast(F32), 0.0)
+        zero_codes = keep.tile([P, P], U32, align_bytes=64)
+        zero_scales = keep.tile([P, P], U8, align_bytes=64)
+        nc.vector.quantize_mx(out=zero_codes[:].bitcast(FP8X4), scales=zero_scales[:], in_=zeros[:])
+        idle_sums = sums.tile([P, P], F32, tag="spare")
+
+        def idle_passes(count):
+            for n in range(count):
+                nc.tensor.matmul_mx(
+                    out=idle_sums[:],
+                    lhsT=zero_codes[:].bitcast(FP8X4),
+                    lhsT_scale=zero_scales[:],
+                    rhs=zero_codes[:].bitcast(FP8X4),
+                    rhs_scale=zero_scales[:],
+                    start=(n == 0),
+                    stop=(n == count - 1),
+                )
+
+        idle_passes(WARM_PASSES)
+
+        nc.vector.memset(s4_row[:].bitcast(F32), 0.0)
+        nc.vector.memset(bias_row[:].bitcast(F32), 0.0)
+        nc.vector.memset(ones[:], 1.0)
 
         s0_cols = keep.tile([P, PASSES * PACK], BF16)
         s2_cols = keep.tile([P, PASSES * PACK], BF16)
@@ -186,6 +211,8 @@ def tile_doublebinarylinear_s_kernel(tc, x, scaling0, B, scaling2, A, scaling4, 
             if w == X_BEFORE:
                 make_h0()
             grouped = regroup(transpose_rows(w_sb[w][:]))
+            if w in IDLE_AFTER:
+                idle_passes(IDLE_PASSES)
             if w == MULTIPLY_AFTER[1]:
                 for n in range(PACK):
                     first_matmul(PACK + n)
@@ -201,7 +228,7 @@ def tile_doublebinarylinear_s_kernel(tc, x, scaling0, B, scaling2, A, scaling4, 
         s4_all = keep.tile([P, OUT_DIM], F32)
         nc.scalar.copy(out=s4_all[:], in_=s4_bank[:])
         first_half = second_matmul(0)
-        bias_all = sums.tile([P, OUT_DIM], F32)
+        bias_all = sums.tile([P, OUT_DIM], F32, tag="spare")
         nc.tensor.matmul(out=bias_all[:], lhsT=ones[:], rhs=bias_row[:], start=True, stop=True)
         quantise(TILES - 1, last_grouped)
         scale_out(0, first_half)

@@ -22,12 +22,9 @@ TILES = B_TILES + A_TILES
 TILE_WORDS = PASSES * P
 STORE_TILES = 2
 
-X_BEFORE = 3
-SCALINGS_BEFORE = 5
-ROWS_BEFORE = 9
 MULTIPLY_AFTER = (6, 9)
 WARM_PASSES = 12
-IDLE_AFTER = (1, 2, 4, 8)
+IDLE_AFTER = (1, 3)
 IDLE_PASSES = 4
 
 FLOPS = 2 * P * K_DIM * K_DIM + 2 * P * K_DIM * OUT_DIM
@@ -41,9 +38,9 @@ def tile_doublebinarylinear_s_kernel(tc, x, scaling0, B, scaling2, A, scaling4, 
     nc = tc.nc
     x_rows = x.rearrange("b s k -> (b s) k")
     out_rows = out.rearrange("b s o -> (b s) o")
-    B_rows = B.rearrange("(g p t) k -> g t p k", g=PASSES, t=PACK)
-    w_rows = [B_rows[w // PACK, w % PACK] for w in range(B_TILES)]
-    w_rows += [A[a * P : (a + 1) * P, :] for a in range(A_TILES)]
+    B_rows = B.rearrange("(g p u e) k -> g u p e k", g=PASSES, u=2, e=2)
+    A_rows = A.rearrange("(c e p) k -> c p e k", e=2, p=P)
+    pair_rows = [B_rows[n // 2, n % 2] for n in range(B_TILES // 2)] + [A_rows[n] for n in range(A_TILES // 2)]
 
     with ExitStack() as ctx:
         keep = ctx.enter_context(tc.tile_pool(name="keep", bufs=1))
@@ -85,21 +82,20 @@ def tile_doublebinarylinear_s_kernel(tc, x, scaling0, B, scaling2, A, scaling4, 
 
         s0_cols = keep.tile([P, PASSES * PACK], BF16)
         s2_cols = keep.tile([P, PASSES * PACK], BF16)
+        for s_cols, scaling in ((s0_cols, scaling0), (s2_cols, scaling2)):
+            nc.scalar.dma_start(
+                out=s_cols[:].rearrange("p (g t) -> p g t", t=PACK),
+                in_=scaling.rearrange("(g p t) -> p g t", p=P, t=PACK),
+            )
+        nc.scalar.dma_start(out=s4_row[0:1, :], in_=scaling4.unsqueeze(0))
+        nc.scalar.dma_start(out=bias_row[0:1, :], in_=bias.unsqueeze(0))
         x_sb = keep.tile([P, K_DIM], BF16)
-        w_sb = [keep.tile([P, K_DIM], BF16, name="w_sb%d" % w) for w in range(TILES)]
-        for w in range(TILES):
-            if w == X_BEFORE:
-                nc.sync.dma_start(out=x_sb[:], in_=x_rows)
-            if w == SCALINGS_BEFORE:
-                for s_cols, scaling in ((s0_cols, scaling0), (s2_cols, scaling2)):
-                    nc.scalar.dma_start(
-                        out=s_cols[:].rearrange("p (g t) -> p g t", t=PACK),
-                        in_=scaling.rearrange("(g p t) -> p g t", p=P, t=PACK),
-                    )
-            if w == ROWS_BEFORE:
-                nc.sync.dma_start(out=s4_row[0:1, :], in_=scaling4.unsqueeze(0))
-                nc.sync.dma_start(out=bias_row[0:1, :], in_=bias.unsqueeze(0))
-            nc.sync.dma_start(out=w_sb[w][:], in_=w_rows[w])
+        nc.sync.dma_start(out=x_sb[:], in_=x_rows)
+        pairs = [keep.tile([P, 2, K_DIM], BF16, name="pair%d" % n) for n in range(TILES // 2)]
+        for n in range(TILES // 2 - 1):
+            nc.sync.dma_start(out=pairs[n][:], in_=pair_rows[n])
+        for e in range(2):
+            nc.sync.dma_start(out=pairs[-1][:, e, :], in_=pair_rows[-1][:, e, :])
 
         def transpose_rows(rows):
             words = rows.bitcast(F32)
@@ -207,10 +203,9 @@ def tile_doublebinarylinear_s_kernel(tc, x, scaling0, B, scaling2, A, scaling4, 
             nc.vector.tensor_tensor(out=results[c][:], in0=results[c][:], in1=bias_all[:, out_cols(c)], op=ADD)
             nc.sync.dma_start(out=out_rows[:, out_cols(c)], in_=results[c][:])
 
+        make_h0()
         for w in range(TILES - 1):
-            if w == X_BEFORE:
-                make_h0()
-            grouped = regroup(transpose_rows(w_sb[w][:]))
+            grouped = regroup(transpose_rows(pairs[w // 2][:, w % 2, :]))
             if w in IDLE_AFTER:
                 idle_passes(IDLE_PASSES)
             if w == MULTIPLY_AFTER[1]:
@@ -222,7 +217,7 @@ def tile_doublebinarylinear_s_kernel(tc, x, scaling0, B, scaling2, A, scaling4, 
                 for n in range(PACK):
                     first_matmul(n)
                 make_h2(0)
-        last_grouped = regroup(transpose_rows(w_sb[TILES - 1][:]))
+        last_grouped = regroup(transpose_rows(pairs[-1][:, 1, :]))
         s4_bank = banks.tile([P, OUT_DIM], F32, name="bank")
         nc.tensor.matmul(out=s4_bank[:], lhsT=ones[:], rhs=s4_row[:], start=True, stop=True)
         s4_all = keep.tile([P, OUT_DIM], F32)

@@ -22,9 +22,8 @@ TILES = B_TILES + A_TILES
 TILE_WORDS = PASSES * P
 STORE_TILES = 2
 
-MULTIPLY_AFTER = (6, 9)
+LOOKAHEAD = 2
 WARM_PASSES = 12
-IDLE_AFTER = (1, 3)
 IDLE_PASSES = 4
 
 FLOPS = 2 * P * K_DIM * K_DIM + 2 * P * K_DIM * OUT_DIM
@@ -204,20 +203,20 @@ def tile_doublebinarylinear_s_kernel(tc, x, scaling0, B, scaling2, A, scaling4, 
             nc.sync.dma_start(out=out_rows[:, out_cols(c)], in_=results[c][:])
 
         make_h0()
-        for w in range(TILES - 1):
-            grouped = regroup(transpose_rows(pairs[w // 2][:, w % 2, :]))
-            if w in IDLE_AFTER:
+        for step in range(TILES // 2):
+            tiles = (2 * step, 2 * step + 1)
+            grouped = [regroup(transpose_rows(pairs[step][:, w % 2, :])) for w in tiles]
+            if step < LOOKAHEAD:
                 idle_passes(IDLE_PASSES)
-            if w == MULTIPLY_AFTER[1]:
-                for n in range(PACK):
-                    first_matmul(PACK + n)
-                make_h2(1)
-            quantise(w, grouped)
-            if w == MULTIPLY_AFTER[0]:
-                for n in range(PACK):
-                    first_matmul(n)
-                make_h2(0)
-        last_grouped = regroup(transpose_rows(pairs[-1][:, 1, :]))
+            else:
+                for w in tiles:
+                    first_matmul(w - 2 * LOOKAHEAD)
+                if step % 2 == 1:
+                    make_h2((step - LOOKAHEAD) // 2)
+            for n in range(2):
+                if tiles[n] < TILES - 1:
+                    quantise(tiles[n], grouped[n])
+        last_grouped = grouped[1]
         s4_bank = banks.tile([P, OUT_DIM], F32, name="bank")
         nc.tensor.matmul(out=s4_bank[:], lhsT=ones[:], rhs=s4_row[:], start=True, stop=True)
         s4_all = keep.tile([P, OUT_DIM], F32)

@@ -22,6 +22,8 @@ TILES = B_TILES + A_TILES
 TILE_WORDS = PASSES * P
 STORE_TILES = 2
 
+RUN = 2
+VECTOR_REGROUPS = (3, 5)
 LOOKAHEAD = 2
 WARM_PASSES = 12
 IDLE_PASSES = 4
@@ -98,11 +100,11 @@ def tile_doublebinarylinear_s_kernel(tc, x, scaling0, B, scaling2, A, scaling4, 
 
         def transpose_rows(rows):
             words = rows.bitcast(F32)
-            bank = banks.tile([P, PASSES, 2, P], F32, name="bank")
+            bank = banks.tile([P, 2, PASSES, P], F32, name="bank")
             for g in range(PASSES):
                 for u in range(2):
                     pass_words = slice(2 * P * g + u, 2 * P * (g + 1), 2)
-                    nc.tensor.transpose(bank[:, g, u, :], words[:, pass_words], identity[:])
+                    nc.tensor.transpose(bank[:, u, g, :], words[:, pass_words], identity[:])
             return bank
 
         h0_codes = keep.tile([P, TILE_WORDS], U32, align_bytes=64)
@@ -110,8 +112,8 @@ def tile_doublebinarylinear_s_kernel(tc, x, scaling0, B, scaling2, A, scaling4, 
 
         def make_h0():
             x_bank = transpose_rows(x_sb[:])
-            x_pairs = x_bank[:].rearrange("p g u r -> p (g u r)").bitcast(BF16)
-            x_pairs = x_pairs.rearrange("p (g u r e) -> p g r u e", g=PASSES, u=2, e=2)
+            x_pairs = x_bank[:].rearrange("p u g r -> p (u g r)").bitcast(BF16)
+            x_pairs = x_pairs.rearrange("p (u g r e) -> p g r u e", g=PASSES, u=2, e=2)
             h0_grouped = keep.tile([P, PASSES, P, PACK], BF16, align_bytes=64)
             for g in range(PASSES):
                 nc.vector.tensor_tensor(
@@ -132,9 +134,13 @@ def tile_doublebinarylinear_s_kernel(tc, x, scaling0, B, scaling2, A, scaling4, 
         w_codes = [keep.tile([P, TILE_WORDS], U32, name="w_codes%d" % w, align_bytes=64) for w in range(TILES)]
         w_scales = [keep.tile([P, TILE_WORDS], U8, name="w_scales%d" % w, align_bytes=64) for w in range(TILES)]
 
-        def regroup(bank):
+        def regroup(w, bank):
             grouped = stage.tile([P, PASSES, P, PACK], BF16, align_bytes=64)
-            nc.scalar.copy(out=grouped[:].bitcast(F32), in_=bank[:].rearrange("p g u r -> p g r u"))
+            copy = nc.vector.tensor_copy if w in VECTOR_REGROUPS else nc.scalar.copy
+            copy(
+                out=grouped[:].rearrange("p g r t -> p (g r t)").bitcast(F32).rearrange("p (c i u) -> p c u i", i=RUN, u=2),
+                in_=bank[:].rearrange("p u g r -> p u (g r)").rearrange("p u (c i) -> p c u i", i=RUN),
+            )
             return grouped
 
         def quantise(w, grouped):
@@ -160,7 +166,7 @@ def tile_doublebinarylinear_s_kernel(tc, x, scaling0, B, scaling2, A, scaling4, 
                     stop=(g == PASSES - 1),
                 )
 
-        def make_h2(g):
+        def scale_h1(g):
             h2_grouped = stage.tile([P, P, PACK], BF16, align_bytes=64)
             nc.vector.tensor_tensor(
                 out=h2_grouped[:],
@@ -168,6 +174,9 @@ def tile_doublebinarylinear_s_kernel(tc, x, scaling0, B, scaling2, A, scaling4, 
                 in1=s2_cols[:, PACK * g : PACK * (g + 1)].unsqueeze(1).to_broadcast([P, P, PACK]),
                 op=MULT,
             )
+            return h2_grouped
+
+        def quantise_h2(g, h2_grouped):
             nc.vector.quantize_mx(
                 out=h2_codes[:, pass_cols(g)].bitcast(FP8X4),
                 scales=h2_scales[:, pass_cols(g)],
@@ -205,17 +214,21 @@ def tile_doublebinarylinear_s_kernel(tc, x, scaling0, B, scaling2, A, scaling4, 
         make_h0()
         for step in range(TILES // 2):
             tiles = (2 * step, 2 * step + 1)
-            grouped = [regroup(transpose_rows(pairs[step][:, w % 2, :])) for w in tiles]
+            w_banks = [transpose_rows(pairs[step][:, n, :]) for n in range(2)]
+            grouped = [regroup(tiles[n], w_banks[n]) for n in range(2)]
             if step < LOOKAHEAD:
                 idle_passes(IDLE_PASSES)
             else:
                 for w in tiles:
                     first_matmul(w - 2 * LOOKAHEAD)
-                if step % 2 == 1:
-                    make_h2((step - LOOKAHEAD) // 2)
-            for n in range(2):
-                if tiles[n] < TILES - 1:
-                    quantise(tiles[n], grouped[n])
+            g, odd = divmod(step - LOOKAHEAD, 2)
+            if g >= 0 and odd:
+                h2_grouped = scale_h1(g)
+            quantise(tiles[0], grouped[0])
+            if g >= 0 and odd:
+                quantise_h2(g, h2_grouped)
+            if tiles[1] < TILES - 1:
+                quantise(tiles[1], grouped[1])
         last_grouped = grouped[1]
         s4_bank = banks.tile([P, OUT_DIM], F32, name="bank")
         nc.tensor.matmul(out=s4_bank[:], lhsT=ones[:], rhs=s4_row[:], start=True, stop=True)
@@ -226,6 +239,6 @@ def tile_doublebinarylinear_s_kernel(tc, x, scaling0, B, scaling2, A, scaling4, 
         nc.tensor.matmul(out=bias_all[:], lhsT=ones[:], rhs=bias_row[:], start=True, stop=True)
         quantise(TILES - 1, last_grouped)
         scale_out(0, first_half)
-        add_bias_and_store(0)
         scale_out(1, second_matmul(1))
+        add_bias_and_store(0)
         add_bias_and_store(1)

@@ -234,9 +234,9 @@ def tile_doublebinarylinear_s_kernel(tc, x, scaling0, B, scaling2, A, scaling4, 
         nc.tensor.matmul(out=s4_bank[:], lhsT=ones[:], rhs=s4_row[:], start=True, stop=True)
         s4_all = keep.tile([P, OUT_DIM], F32)
         nc.scalar.copy(out=s4_all[:], in_=s4_bank[:])
-        first_half = second_matmul(0)
         bias_all = sums.tile([P, OUT_DIM], F32, tag="spare")
         nc.tensor.matmul(out=bias_all[:], lhsT=ones[:], rhs=bias_row[:], start=True, stop=True)
+        first_half = second_matmul(0)
         quantise(TILES - 1, last_grouped)
         scale_out(0, first_half)
         scale_out(1, second_matmul(1))

from contextlib import ExitStack

import concourse.mybir as mybir
from concourse.masks import make_identity

BF16 = mybir.dt.bfloat16
F32 = mybir.dt.float32
U32 = mybir.dt.uint32
U8 = mybir.dt.uint8
FP8X4 = mybir.dt.float8_e4m3fn_x4
MULT = mybir.AluOpType.mult
ADD = mybir.AluOpType.add

P = 128
PACK = 4
PASSES = 2
K_DIM = 1024
OUT_DIM = 512
B_TILES = 8
A_TILES = 4
TILES = B_TILES + A_TILES
TILE_WORDS = PASSES * P
STORE_TILES = 2

RUN = 2
VECTOR_REGROUPS = (3, 5)
LOOKAHEAD = 2
WARM_PASSES = 12
IDLE_PASSES = 4

FLOPS = 2 * P * K_DIM * K_DIM + 2 * P * K_DIM * OUT_DIM


def pass_cols(g):
    return slice(g * P, (g + 1) * P)


def tile_doublebinarylinear_s_kernel(tc, x, scaling0, B, scaling2, A, scaling4, bias, out):
    nc = tc.nc
    x_rows = x.rearrange("b s k -> (b s) k")
    out_rows = out.rearrange("b s o -> (b s) o")
    B_rows = B.rearrange("(g p u e) k -> g u p e k", g=PASSES, u=2, e=2)
    A_rows = A.rearrange("(c e p) k -> c p e k", e=2, p=P)
    pair_rows = [B_rows[n // 2, n % 2] for n in range(B_TILES // 2)] + [A_rows[n] for n in range(A_TILES // 2)]

    with ExitStack() as ctx:
        keep = ctx.enter_context(tc.tile_pool(name="keep", bufs=1))
        stage = ctx.enter_context(tc.tile_pool(name="stage", bufs=4))
        banks = ctx.enter_context(tc.psum_pool(name="banks", bufs=5))
        sums = ctx.enter_context(tc.psum_pool(name="sums", bufs=1))
        ctx.enter_context(tc.manual_schedule())

        s4_row = keep.tile([P, OUT_DIM], BF16)
        bias_row = keep.tile([P, OUT_DIM], BF16)
        ones = keep.tile([P, P], BF16)
        identity = keep.tile([P, P], F32)
        make_identity(nc, identity[:])

        zeros = keep.tile([P, PACK * P], BF16, align_bytes=64)
        nc.vector.memset(zeros[:].bitcast(F32), 0.0)
        zero_codes = keep.tile([P, P], U32, align_bytes=64)
        zero_scales = keep.tile([P, P], U8, align_bytes=64)
        nc.vector.quantize_mx(out=zero_codes[:].bitcast(FP8X4), scales=zero_scales[:], in_=zeros[:])
        idle_sums = sums.tile([P, P], F32, tag="spare")

        def idle_passes(count):
            for n in range(count):
                nc.tensor.matmul_mx(
                    out=idle_sums[:],
                    lhsT=zero_codes[:].bitcast(FP8X4),
                    lhsT_scale=zero_scales[:],
                    rhs=zero_codes[:].bitcast(FP8X4),
                    rhs_scale=zero_scales[:],
                    start=(n == 0),
                    stop=(n == count - 1),
                )

        idle_passes(WARM_PASSES)

        nc.vector.memset(s4_row[:].bitcast(F32), 0.0)
        nc.vector.memset(bias_row[:].bitcast(F32), 0.0)
        nc.vector.memset(ones[:], 1.0)

        s0_cols = keep.tile([P, PASSES * PACK], BF16)
        s2_cols = keep.tile([P, PASSES * PACK], BF16)
        for s_cols, scaling in ((s0_cols, scaling0), (s2_cols, scaling2)):
            nc.scalar.dma_start(
                out=s_cols[:].rearrange("p (g t) -> p g t", t=PACK),
                in_=scaling.rearrange("(g p t) -> p g t", p=P, t=PACK),
            )
        nc.scalar.dma_start(out=s4_row[0:1, :], in_=scaling4.unsqueeze(0))
        nc.scalar.dma_start(out=bias_row[0:1, :], in_=bias.unsqueeze(0))
        x_sb = keep.tile([P, K_DIM], BF16)
        nc.sync.dma_start(out=x_sb[:], in_=x_rows)
        pairs = [keep.tile([P, 2, K_DIM], BF16, name="pair%d" % n) for n in range(TILES // 2)]
        for n in range(TILES // 2 - 1):
            nc.sync.dma_start(out=pairs[n][:], in_=pair_rows[n])
        for e in range(2):
            nc.sync.dma_start(out=pairs[-1][:, e, :], in_=pair_rows[-1][:, e, :])

        def transpose_rows(rows):
            words = rows.bitcast(F32)
            bank = banks.tile([P, 2, PASSES, P], F32, name="bank")
            for g in range(PASSES):
                for u in range(2):
                    pass_words = slice(2 * P * g + u, 2 * P * (g + 1), 2)
                    nc.tensor.transpose(bank[:, u, g, :], words[:, pass_words], identity[:])
            return bank

        h0_codes = keep.tile([P, TILE_WORDS], U32, align_bytes=64)
        h0_scales = keep.tile([P, TILE_WORDS], U8, align_bytes=64)

        def make_h0():
            x_bank = transpose_rows(x_sb[:])
            x_pairs = x_bank[:].rearrange("p u g r -> p (u g r)").bitcast(BF16)
            x_pairs = x_pairs.rearrange("p (u g r e) -> p g r u e", g=PASSES, u=2, e=2)
            h0_grouped = keep.tile([P, PASSES, P, PACK], BF16, align_bytes=64)
            for g in range(PASSES):
                nc.vector.tensor_tensor(
                    out=h0_grouped[:, g].rearrange("p r (u e) -> p r u e", e=2),
                    in0=x_pairs[:, g],
                    in1=s0_cols[:, PACK * g : PACK * (g + 1)]
                    .rearrange("p (u e) -> p u e", e=2)
                    .unsqueeze(1)
                    .to_broadcast([P, P, 2, 2]),
                    op=MULT,
                )
            nc.vector.quantize_mx(
                out=h0_codes[:].bitcast(FP8X4),
                scales=h0_scales[:],
                in_=h0_grouped[:].rearrange("p g r t -> p (g r t)"),
            )

        w_codes = [keep.tile([P, TILE_WORDS], U32, name="w_codes%d" % w, align_bytes=64) for w in range(TILES)]
        w_scales = [keep.tile([P, TILE_WORDS], U8, name="w_scales%d" % w, align_bytes=64) for w in range(TILES)]

        def regroup(w, bank):
            grouped = stage.tile([P, PASSES, P, PACK], BF16, align_bytes=64)
            copy = nc.vector.tensor_copy if w in VECTOR_REGROUPS else nc.scalar.copy
            copy(
                out=grouped[:].rearrange("p g r t -> p (g r t)").bitcast(F32).rearrange("p (c i u) -> p c u i", i=RUN, u=2),
                in_=bank[:].rearrange("p u g r -> p u (g r)").rearrange("p u (c i) -> p c u i", i=RUN),
            )
            return grouped

        def quantise(w, grouped):
            nc.vector.quantize_mx(
                out=w_codes[w][:].bitcast(FP8X4),
                scales=w_scales[w][:],
                in_=grouped[:].rearrange("p g r t -> p (g r t)"),
            )

        h1 = [sums.tile([P, PACK, P], F32, name="h1_%d" % g) for g in range(PASSES)]
        h2_codes = keep.tile([P, TILE_WORDS], U32, align_bytes=64)
        h2_scales = keep.tile([P, TILE_WORDS], U8, align_bytes=64)

        def first_matmul(w):
            for g in range(PASSES):
                nc.tensor.matmul_mx(
                    out=h1[w // PACK][:, w % PACK, :],
                    lhsT=w_codes[w][:, pass_cols(g)].bitcast(FP8X4),
                    lhsT_scale=w_scales[w][:, pass_cols(g)],
                    rhs=h0_codes[:, pass_cols(g)].bitcast(FP8X4),
                    rhs_scale=h0_scales[:, pass_cols(g)],
                    start=(g == 0),
                    stop=(g == PASSES - 1),
                )

        def scale_h1(g):
            h2_grouped = stage.tile([P, P, PACK], BF16, align_bytes=64)
            nc.vector.tensor_tensor(
                out=h2_grouped[:],
                in0=h1[g][:].rearrange("p t r -> p r t"),
                in1=s2_cols[:, PACK * g : PACK * (g + 1)].unsqueeze(1).to_broadcast([P, P, PACK]),
                op=MULT,
            )
            return h2_grouped

        def quantise_h2(g, h2_grouped):
            nc.vector.quantize_mx(
                out=h2_codes[:, pass_cols(g)].bitcast(FP8X4),
                scales=h2_scales[:, pass_cols(g)],
                in_=h2_grouped[:].rearrange("p r t -> p (r t)"),
            )

        def second_matmul(c):
            h3 = banks.tile([P, STORE_TILES * P], F32, name="bank")
            for n in range(STORE_TILES):
                w = B_TILES + STORE_TILES * c + n
                for g in range(PASSES):
                    nc.tensor.matmul_mx(
                        out=h3[:, n * P : (n + 1) * P],
                        lhsT=h2_codes[:, pass_cols(g)].bitcast(FP8X4),
                        lhsT_scale=h2_scales[:, pass_cols(g)],
                        rhs=w_codes[w][:, pass_cols(g)].bitcast(FP8X4),
                        rhs_scale=w_scales[w][:, pass_cols(g)],
                        start=(g == 0),
                        stop=(g == PASSES - 1),
                    )
            return h3

        results = [keep.tile([P, STORE_TILES * P], F32, name="result%d" % c) for c in range(A_TILES // STORE_TILES)]

        def out_cols(c):
            return slice(c * STORE_TILES * P, (c + 1) * STORE_TILES * P)

        def scale_out(c, h3):
            nc.vector.tensor_tensor(out=results[c][:], in0=h3[:], in1=s4_all[:, out_cols(c)], op=MULT)

        def add_bias_and_store(c):
            nc.vector.tensor_tensor(out=results[c][:], in0=results[c][:], in1=bias_all[:, out_cols(c)], op=ADD)
            nc.sync.dma_start(out=out_rows[:, out_cols(c)], in_=results[c][:])

        make_h0()
        for step in range(TILES // 2):
            tiles = (2 * step, 2 * step + 1)
            w_banks = [transpose_rows(pairs[step][:, n, :]) for n in range(2)]
            grouped = [regroup(tiles[n], w_banks[n]) for n in range(2)]
            if step < LOOKAHEAD:
                idle_passes(IDLE_PASSES)
            else:
                for w in tiles:
                    first_matmul(w - 2 * LOOKAHEAD)
            g, odd = divmod(step - LOOKAHEAD, 2)
            if g >= 0 and odd:
                h2_grouped = scale_h1(g)
            quantise(tiles[0], grouped[0])
            if g >= 0 and odd:
                quantise_h2(g, h2_grouped)
            if tiles[1] < TILES - 1:
                quantise(tiles[1], grouped[1])
        last_grouped = grouped[1]
        s4_bank = banks.tile([P, OUT_DIM], F32, name="bank")
        nc.tensor.matmul(out=s4_bank[:], lhsT=ones[:], rhs=s4_row[:], start=True, stop=True)
        s4_all = keep.tile([P, OUT_DIM], F32)
        nc.scalar.copy(out=s4_all[:], in_=s4_bank[:])
        bias_all = sums.tile([P, OUT_DIM], F32, tag="spare")
        nc.tensor.matmul(out=bias_all[:], lhsT=ones[:], rhs=bias_row[:], start=True, stop=True)
        first_half = second_matmul(0)
        quantise(TILES - 1, last_grouped)
        scale_out(0, first_half)
        scale_out(1, second_matmul(1))
        add_bias_and_store(0)
        add_bias_and_store(1)
